import numpy as np
import ml_dtypes


def mxq(x, axis, fmt="e4m3"):
    dtype, down = {"e4m3": (ml_dtypes.float8_e4m3fn, 7), "e5m2": (ml_dtypes.float8_e5m2, 14)}[fmt]
    v = np.moveaxis(np.asarray(x, np.float32).astype(ml_dtypes.bfloat16).astype(np.float64), axis, -1)
    blocks = v.reshape(v.shape[:-1] + (-1, 32))
    amax = np.abs(blocks).max(-1, keepdims=True)
    byte = np.maximum(np.where(amax > 0, np.frexp(amax)[1] - 1 + 127, 0) - down, 1)
    scale = np.exp2(byte - 127.0)
    codes = (blocks / scale).astype(np.float32).astype(dtype).astype(np.float64)
    return np.moveaxis((codes * scale).reshape(v.shape), -1, axis)


WIDE = False


def mx_kscale(k):
    if not WIDE:
        return np.ones(k)
    levels = np.array([10, -10, 5, -5, 0])
    a = np.random.permutation(np.resize(levels, k // 512 * 4)).reshape(k // 512, 4)
    idx = np.arange(k)
    return np.exp2(a[idx // 512, idx % 128 // 32])


BF16 = ml_dtypes.bfloat16


def bf(x):
    return np.asarray(x, np.float32).astype(BF16)


def f64(x):
    return np.asarray(x).astype(np.float64)


E2M1 = np.array([0.0, 0.5, 1.0, 1.5, 2.0, 3.0, 4.0, 6.0, -0.0, -0.5, -1.0, -1.5, -2.0, -3.0, -4.0, -6.0])


def pack_weight(w, fmt):
    k, n = w.shape
    w = f64(bf(w)).reshape(k // 32, 32, n)
    amax = np.abs(w).max(1)
    if fmt == "e4m3":
        byte = np.frexp(amax)[1] - 1 + 127 - 7
    else:
        mant, ex = np.frexp(amax / 6.0)
        byte = np.where(mant > 0.5, ex, ex - 1) + 127
    byte = np.clip(np.where(amax > 0, byte, 1), 1, 254)
    scaled = (w * np.exp2(127.0 - byte)[:, None, :]).reshape(k, n).astype(np.float32)
    by_word = np.ascontiguousarray(scaled.reshape(k // 512, 128, 4, n).transpose(0, 1, 3, 2))
    if fmt == "e4m3":
        words = by_word.astype(ml_dtypes.float8_e4m3fn).view(np.uint8)
    else:
        c = by_word.astype(ml_dtypes.float4_e2m1fn).view(np.uint8) & 0xF
        words = c[..., 0::2] | (c[..., 1::2] << 4)
    return np.ascontiguousarray(words), np.ascontiguousarray(byte.astype(np.uint8).reshape(k // 512, 16, n))


def unpack_weight(words, scales, fmt):
    g, p, n, _ = words.shape
    if fmt == "e4m3":
        vals = np.ascontiguousarray(words).view(ml_dtypes.float8_e4m3fn).astype(np.float64)
    else:
        nib = np.empty((g, p, n, 4), np.uint8)
        nib[..., 0::2] = words & 0xF
        nib[..., 1::2] = words >> 4
        vals = E2M1[nib]
    vals = vals * np.repeat(np.exp2(scales.astype(np.float64) - 127.0), 8, axis=1)[..., None]
    return vals.transpose(0, 1, 3, 2).reshape(g * 512, n)

def pack4(w):
    words, scales = pack_weight(w, "e2m1")
    return words.reshape(words.shape[0], 128, -1), scales


def unpack4(words, scales):
    return unpack_weight(words.reshape(words.shape[0], 128, -1, 2), scales, "e2m1")


B, HW, C, HID, WS, SS, HEADS = 1, 16, 1024, 2048, 8, 4, 16
L = HW * HW
NH = HW // WS
EPS = 1e-5


def adain(x, scale, shift):
    m = x.mean(2, keepdims=True)
    s = np.std(x, axis=2, keepdims=True, ddof=1) + EPS
    return (x - m) / s * scale + shift


def setup_inputs():
    s = mx_kscale(C)
    o_attn = bf(0.4 * np.random.standard_normal((NH * NH * B, WS * WS, C)) * s)
    out_w = np.random.standard_normal((C, C)) / np.sqrt(C) / s[None, :]
    words, scales = pack4(np.ascontiguousarray(out_w.T))
    return {"o_attn": o_attn,
            "out_w_words": words,
            "out_w_scales": scales,
            "out_b": bf(0.1 * np.random.standard_normal(C)),
            "ada1_scale": bf(1.0 + 0.1 * np.random.standard_normal((1, L, 1))),
            "ada1_shift": bf(0.1 * np.random.standard_normal((1, L, 1))),
            "x": bf(np.random.standard_normal((B, L, C)))}


def reference(o_attn, out_w_words, out_w_scales, out_b, ada1_scale, ada1_shift, x):
    a = (mxq(f64(o_attn), 2, "e4m3") @ unpack4(out_w_words, out_w_scales)) + f64(out_b)
    a = np.swapaxes(a.reshape(B, NH, NH, WS, WS, C), 2, 3).reshape(B, HW, HW, C)
    a = np.roll(a, (SS, SS), axis=(1, 2)).reshape(B, L, C)
    return f64(x) + adain(a, f64(ada1_scale), f64(ada1_shift))

@@ -1,0 +1,234 @@
+from contextlib import ExitStack
+
+import concourse.mybir as mybir
+from concourse.masks import make_identity
+
+F32 = mybir.dt.float32
+BF16 = mybir.dt.bfloat16
+I32 = mybir.dt.int32
+U32 = mybir.dt.uint32
+U8 = mybir.dt.uint8
+FP8X4 = mybir.dt.float8_e4m3fn_x4
+FP4X4 = mybir.dt.float4_e2m1fn_x4
+ALU = mybir.AluOpType
+ACT = mybir.ActivationFunctionType
+
+P = 128
+GRID = 16
+WIN = 8
+SHIFT = 4
+TOKENS = GRID * GRID
+CHANNELS = 1024
+EPS = 1e-5
+
+TILES = TOKENS // P
+K_PASS = 4 * P
+PASSES = CHANNELS // K_PASS
+BANK = 512
+BANKS = CHANNELS // BANK
+
+FLOPS = 2 * TOKENS * CHANNELS * CHANNELS
+
+
+def token_runs(s):
+    first = P * s + SHIFT * GRID
+    if first + P <= TOKENS:
+        return [(0, first, P)]
+    head = TOKENS - first
+    return [(0, first, head), (head, 0, P - head)]
+
+
+def tile_swintransformerblock_pb_s_kernel(
+    tc, o_attn, out_w_words, out_w_scales, out_b, ada1_scale, ada1_shift, x, out
+):
+    nc = tc.nc
+    with ExitStack() as ctx:
+        keep = ctx.enter_context(tc.tile_pool(name="keep", bufs=1))
+        psum = ctx.enter_context(tc.psum_pool(name="psum", bufs=1))
+
+        def one_per_tile(pool, shape, dtype, name, align_bytes=None):
+            return [
+                pool.tile(shape, dtype, name="%s%d" % (name, s), align_bytes=align_bytes)
+                for s in range(TILES)
+            ]
+
+        tile_order = [1, 0]
+
+        o_rows = o_attn.rearrange("w t c -> (w t) c")
+        o_sb = one_per_tile(keep, [P, CHANNELS], BF16, "o_sb")
+        for s in tile_order:
+            nc.sync.dma_start(out=o_sb[s][:], in_=o_rows[P * s : P * (s + 1), :])
+
+        bias_rows = keep.tile([P, CHANNELS], BF16)
+        nc.vector.memset(bias_rows[:].bitcast(I32), 0)
+        nc.scalar.dma_start(out=bias_rows[0:1, :], in_=out_b.rearrange("(o c) -> o c", o=1))
+        ones = keep.tile([P, P], BF16)
+        nc.vector.memset(ones[:], 1.0)
+
+        w_scales = keep.tile([P, PASSES, CHANNELS], U8, align_bytes=64)
+        nc.vector.memset(w_scales[:].bitcast(I32), 0)
+        for r in range(4):
+            nc.sync.dma_start(
+                out=w_scales[r:P:32, :, :].bitcast(I32),
+                in_=out_w_scales[:, r:16:4, :].rearrange("g q n -> q g n").bitcast(I32),
+            )
+        w_words = keep.tile([P, PASSES, 2 * CHANNELS], U8, align_bytes=64)
+        nc.sync.dma_start(
+            out=w_words[:].bitcast(I32),
+            in_=out_w_words.rearrange("g p b -> p g b").bitcast(I32),
+        )
+
+        x_sb = one_per_tile(keep, [P, CHANNELS], BF16, "x_sb")
+        gain_bf = one_per_tile(keep, [P, 1], BF16, "gain_bf")
+        offset_bf = one_per_tile(keep, [P, 1], BF16, "offset_bf")
+        for s in tile_order:
+            for p0, t0, count in token_runs(s):
+                nc.sync.dma_start(out=x_sb[s][p0 : p0 + count, :], in_=x[0, t0 : t0 + count, :])
+                with nc.allow_non_contiguous_dma(reason="one 2-byte value for each partition"):
+                    nc.scalar.dma_start(
+                        out=offset_bf[s][p0 : p0 + count, :], in_=ada1_shift[0, t0 : t0 + count, :]
+                    )
+                    nc.scalar.dma_start(
+                        out=gain_bf[s][p0 : p0 + count, :], in_=ada1_scale[0, t0 : t0 + count, :]
+                    )
+
+        one_col = keep.tile([P, 1], F32)
+        nc.vector.memset(one_col[:], 1.0)
+        sqrt_warm = keep.tile([P, 1], F32)
+        nc.scalar.activation(out=sqrt_warm[:], in_=one_col[:], func=ACT.Sqrt)
+
+        ident = keep.tile([P, P], F32)
+        make_identity(nc, ident[:])
+        perm = keep.tile([P, P], F32)
+        by_window = ident[:].rearrange("p (wj r c) -> p wj r c", wj=2, r=WIN)
+        by_image_row = perm[:].rearrange("p (r j) -> p r j", j=GRID)
+        nc.vector.tensor_copy(out=by_image_row[:, :, SHIFT : SHIFT + WIN], in_=by_window[:, 0, :, :])
+        nc.vector.tensor_copy(
+            out=by_image_row[:, :, SHIFT + WIN : GRID], in_=by_window[:, 1, :, 0 : WIN - SHIFT]
+        )
+        nc.vector.tensor_copy(out=by_image_row[:, :, 0:SHIFT], in_=by_window[:, 1, :, WIN - SHIFT : WIN])
+
+        transposed = one_per_tile(psum, [P, PASSES, 2, P], F32, "transposed")
+        grouped = one_per_tile(keep, [P, PASSES * P * 4], BF16, "grouped", align_bytes=64)
+        a_words = one_per_tile(keep, [P, PASSES * P], U32, "a_words", align_bytes=64)
+        a_scales = one_per_tile(keep, [P, PASSES * P], U8, "a_scales", align_bytes=64)
+        for s in tile_order:
+            o_pairs = o_sb[s][:].bitcast(F32)
+            for g in range(PASSES):
+                for u in range(2):
+                    nc.tensor.transpose(
+                        transposed[s][:, g, u, :],
+                        o_pairs[:, 2 * P * g + u : 2 * P * (g + 1) : 2],
+                        perm[:],
+                    )
+            nc.scalar.copy(
+                out=grouped[s][:].bitcast(F32).rearrange("p (g n u) -> p g n u", g=PASSES, u=2),
+                in_=transposed[s][:].rearrange("p g u n -> p g n u"),
+            )
+
+        bias_ps = psum.tile([P, CHANNELS], BF16)
+        for h in range(BANKS):
+            cols = slice(BANK * h, BANK * (h + 1))
+            nc.tensor.matmul(
+                out=bias_ps[:, cols], lhsT=ones[:], rhs=bias_rows[:, cols], start=True, stop=True
+            )
+        bias_all = keep.tile([P, CHANNELS], BF16)
+        nc.vector.tensor_copy(out=bias_all[:], in_=bias_ps[:])
+
+        for s in tile_order:
+            nc.vector.quantize_mx(
+                out=a_words[s][:].bitcast(FP8X4), scales=a_scales[s][:], in_=grouped[s][:]
+            )
+
+        acc = [
+            [psum.tile([P, BANK], F32, name="acc%d%d" % (s, h)) for h in range(BANKS)]
+            for s in range(TILES)
+        ]
+        for s in tile_order:
+            for h in range(BANKS):
+                for g in range(PASSES):
+                    nc.tensor.matmul_mx(
+                        out=acc[s][h][:],
+                        lhsT=a_words[s][:, P * g : P * (g + 1)].bitcast(FP8X4),
+                        lhsT_scale=a_scales[s][:, P * g : P * (g + 1)],
+                        rhs=w_words[:, g, 2 * BANK * h : 2 * BANK * (h + 1)].bitcast(FP4X4),
+                        rhs_scale=w_scales[:, g, BANK * h : BANK * (h + 1)],
+                        start=(g == 0),
+                        stop=(g == PASSES - 1),
+                    )
+
+        gain = one_per_tile(keep, [P, 1], F32, "gain")
+        offset = one_per_tile(keep, [P, 1], F32, "offset")
+        x_offset = one_per_tile(keep, [P, CHANNELS], F32, "x_offset")
+        for s in tile_order:
+            nc.vector.tensor_copy(out=gain[s][:], in_=gain_bf[s][:])
+            nc.vector.tensor_copy(out=offset[s][:], in_=offset_bf[s][:])
+            nc.scalar.activation(
+                out=x_offset[s][:], in_=x_sb[s][:], func=ACT.Identity, bias=offset[s][:], scale=1.0
+            )
+
+        a_sb = one_per_tile(keep, [P, CHANNELS], F32, "a_sb")
+        row_sums = one_per_tile(keep, [P, BANKS], F32, "row_sums")
+        neg_mean = one_per_tile(keep, [P, 1], F32, "neg_mean")
+        squares = one_per_tile(keep, [P, CHANNELS], F32, "squares")
+        sum_squares = one_per_tile(keep, [P, 1], F32, "sum_squares")
+        centred = one_per_tile(keep, [P, CHANNELS], F32, "centred")
+        std = one_per_tile(keep, [P, 1], F32, "std")
+        std_eps = one_per_tile(keep, [P, 1], F32, "std_eps")
+        inv_std = one_per_tile(keep, [P, 1], F32, "inv_std")
+        result = one_per_tile(keep, [P, CHANNELS], F32, "result")
+        for s in tile_order:
+            for h in range(BANKS):
+                cols = slice(BANK * h, BANK * (h + 1))
+                nc.vector.scalar_tensor_tensor(
+                    out=a_sb[s][:, cols],
+                    in0=acc[s][h][:],
+                    scalar=1.0,
+                    in1=bias_all[:, cols],
+                    op0=ALU.mult,
+                    op1=ALU.add,
+                    accum_out=row_sums[s][:, h : h + 1],
+                )
+            nc.vector.tensor_scalar(
+                out=neg_mean[s][:],
+                in0=row_sums[s][:, 0:1],
+                scalar1=row_sums[s][:, 1:2],
+                scalar2=-1.0 / CHANNELS,
+                op0=ALU.add,
+                op1=ALU.mult,
+            )
+            nc.scalar.activation(
+                out=squares[s][:],
+                in_=a_sb[s][:],
+                func=ACT.Square,
+                bias=neg_mean[s][:],
+                scale=1.0,
+                accum_out=sum_squares[s][:],
+            )
+            nc.vector.tensor_scalar(
+                out=centred[s][:],
+                in0=a_sb[s][:],
+                scalar1=neg_mean[s][:],
+                scalar2=gain[s][:],
+                op0=ALU.add,
+                op1=ALU.mult,
+            )
+            nc.scalar.activation(
+                out=std[s][:], in_=sum_squares[s][:], func=ACT.Sqrt, scale=1.0 / (CHANNELS - 1)
+            )
+            nc.vector.tensor_scalar_add(out=std_eps[s][:], in0=std[s][:], scalar1=EPS)
+            nc.vector.reciprocal(out=inv_std[s][:], in_=std_eps[s][:])
+            for h in range(BANKS):
+                cols = slice(BANK * h, BANK * (h + 1))
+                nc.vector.scalar_tensor_tensor(
+                    out=result[s][:, cols],
+                    in0=centred[s][:, cols],
+                    scalar=inv_std[s][:],
+                    in1=x_offset[s][:, cols],
+                    op0=ALU.mult,
+                    op1=ALU.add,
+                )
+                for p0, t0, count in token_runs(s):
+                    nc.sync.dma_start(
+                        out=out[0, t0 : t0 + count, cols], in_=result[s][p0 : p0 + count, cols]
+                    )

@@ -45,6 +45,7 @@ def tile_swintransformerblock_pb_s_kernel(
     with ExitStack() as ctx:
         keep = ctx.enter_context(tc.tile_pool(name="keep", bufs=1))
         psum = ctx.enter_context(tc.psum_pool(name="psum", bufs=1))
+        ctx.enter_context(tc.manual_schedule())
 
         def one_per_tile(pool, shape, dtype, name, align_bytes=None):
             return [
@@ -62,8 +63,6 @@ def tile_swintransformerblock_pb_s_kernel(
         bias_rows = keep.tile([P, CHANNELS], BF16)
         nc.vector.memset(bias_rows[:].bitcast(I32), 0)
         nc.scalar.dma_start(out=bias_rows[0:1, :], in_=out_b.rearrange("(o c) -> o c", o=1))
-        ones = keep.tile([P, P], BF16)
-        nc.vector.memset(ones[:], 1.0)
 
         w_scales = keep.tile([P, PASSES, CHANNELS], U8, align_bytes=64)
         nc.vector.memset(w_scales[:].bitcast(I32), 0)
@@ -82,16 +81,20 @@ def tile_swintransformerblock_pb_s_kernel(
         gain_bf = one_per_tile(keep, [P, 1], BF16, "gain_bf")
         offset_bf = one_per_tile(keep, [P, 1], BF16, "offset_bf")
         for s in tile_order:
-            for p0, t0, count in token_runs(s):
-                nc.sync.dma_start(out=x_sb[s][p0 : p0 + count, :], in_=x[0, t0 : t0 + count, :])
-                with nc.allow_non_contiguous_dma(reason="one 2-byte value for each partition"):
-                    nc.scalar.dma_start(
-                        out=offset_bf[s][p0 : p0 + count, :], in_=ada1_shift[0, t0 : t0 + count, :]
-                    )
-                    nc.scalar.dma_start(
+            with nc.allow_non_contiguous_dma(reason="one 2-byte value for each partition"):
+                for p0, t0, count in token_runs(s):
+                    nc.sync.dma_start(
                         out=gain_bf[s][p0 : p0 + count, :], in_=ada1_scale[0, t0 : t0 + count, :]
                     )
+                for p0, t0, count in token_runs(s):
+                    nc.sync.dma_start(
+                        out=offset_bf[s][p0 : p0 + count, :], in_=ada1_shift[0, t0 : t0 + count, :]
+                    )
+            for p0, t0, count in token_runs(s):
+                nc.sync.dma_start(out=x_sb[s][p0 : p0 + count, :], in_=x[0, t0 : t0 + count, :])
 
+        ones = keep.tile([P, P], BF16)
+        nc.vector.memset(ones[:], 1.0)
         one_col = keep.tile([P, 1], F32)
         nc.vector.memset(one_col[:], 1.0)
         sqrt_warm = keep.tile([P, 1], F32)
@@ -107,6 +110,15 @@ def tile_swintransformerblock_pb_s_kernel(
             out=by_image_row[:, :, SHIFT + WIN : GRID], in_=by_window[:, 1, :, 0 : WIN - SHIFT]
         )
         nc.vector.tensor_copy(out=by_image_row[:, :, 0:SHIFT], in_=by_window[:, 1, :, WIN - SHIFT : WIN])
+
+        bias_ps = psum.tile([P, CHANNELS], BF16)
+        for h in range(BANKS):
+            cols = slice(BANK * h, BANK * (h + 1))
+            nc.tensor.matmul(
+                out=bias_ps[:, cols], lhsT=ones[:], rhs=bias_rows[:, cols], start=True, stop=True
+            )
+        bias_all = keep.tile([P, CHANNELS], BF16)
+        nc.vector.tensor_copy(out=bias_all[:], in_=bias_ps[:])
 
         transposed = one_per_tile(psum, [P, PASSES, 2, P], F32, "transposed")
         grouped = one_per_tile(keep, [P, PASSES * P * 4], BF16, "grouped", align_bytes=64)
@@ -125,16 +137,6 @@ def tile_swintransformerblock_pb_s_kernel(
                 out=grouped[s][:].bitcast(F32).rearrange("p (g n u) -> p g n u", g=PASSES, u=2),
                 in_=transposed[s][:].rearrange("p g u n -> p g n u"),
             )
-
-        bias_ps = psum.tile([P, CHANNELS], BF16)
-        for h in range(BANKS):
-            cols = slice(BANK * h, BANK * (h + 1))
-            nc.tensor.matmul(
-                out=bias_ps[:, cols], lhsT=ones[:], rhs=bias_rows[:, cols], start=True, stop=True
-            )
-        bias_all = keep.tile([P, CHANNELS], BF16)
-        nc.vector.tensor_copy(out=bias_all[:], in_=bias_ps[:])
-
         for s in tile_order:
             nc.vector.quantize_mx(
                 out=a_words[s][:].bitcast(FP8X4), scales=a_scales[s][:], in_=grouped[s][:]
@@ -157,14 +159,17 @@ def tile_swintransformerblock_pb_s_kernel(
                         stop=(g == PASSES - 1),
                     )
 
-        gain = one_per_tile(keep, [P, 1], F32, "gain")
-        offset = one_per_tile(keep, [P, 1], F32, "offset")
         x_offset = one_per_tile(keep, [P, CHANNELS], F32, "x_offset")
+        gain = one_per_tile(keep, [P, 1], F32, "gain")
         for s in tile_order:
-            nc.vector.tensor_copy(out=gain[s][:], in_=gain_bf[s][:])
-            nc.vector.tensor_copy(out=offset[s][:], in_=offset_bf[s][:])
-            nc.scalar.activation(
-                out=x_offset[s][:], in_=x_sb[s][:], func=ACT.Identity, bias=offset[s][:], scale=1.0
+            nc.gpsimd.tensor_copy(out=gain[s][:], in_=gain_bf[s][:])
+            nc.gpsimd.tensor_scalar(
+                out=x_offset[s][:],
+                in0=x_sb[s][:],
+                scalar1=1.0,
+                scalar2=offset_bf[s][:],
+                op0=ALU.mult,
+                op1=ALU.add,
             )
 
         a_sb = one_per_tile(keep, [P, CHANNELS], F32, "a_sb")
@@ -174,9 +179,6 @@ def tile_swintransformerblock_pb_s_kernel(
         sum_squares = one_per_tile(keep, [P, 1], F32, "sum_squares")
         centred = one_per_tile(keep, [P, CHANNELS], F32, "centred")
         std = one_per_tile(keep, [P, 1], F32, "std")
-        std_eps = one_per_tile(keep, [P, 1], F32, "std_eps")
-        inv_std = one_per_tile(keep, [P, 1], F32, "inv_std")
-        result = one_per_tile(keep, [P, CHANNELS], F32, "result")
         for s in tile_order:
             for h in range(BANKS):
                 cols = slice(BANK * h, BANK * (h + 1))
@@ -205,7 +207,10 @@ def tile_swintransformerblock_pb_s_kernel(
                 scale=1.0,
                 accum_out=sum_squares[s][:],
             )
-            nc.vector.tensor_scalar(
+            nc.scalar.activation(
+                out=std[s][:], in_=sum_squares[s][:], func=ACT.Sqrt, scale=1.0 / (CHANNELS - 1)
+            )
+            nc.gpsimd.tensor_scalar(
                 out=centred[s][:],
                 in0=a_sb[s][:],
                 scalar1=neg_mean[s][:],
@@ -213,9 +218,11 @@ def tile_swintransformerblock_pb_s_kernel(
                 op0=ALU.add,
                 op1=ALU.mult,
             )
-            nc.scalar.activation(
-                out=std[s][:], in_=sum_squares[s][:], func=ACT.Sqrt, scale=1.0 / (CHANNELS - 1)
-            )
+
+        std_eps = one_per_tile(keep, [P, 1], F32, "std_eps")
+        inv_std = one_per_tile(keep, [P, 1], F32, "inv_std")
+        result = one_per_tile(keep, [P, CHANNELS], F32, "result")
+        for s in tile_order:
             nc.vector.tensor_scalar_add(out=std_eps[s][:], in0=std[s][:], scalar1=EPS)
             nc.vector.reciprocal(out=inv_std[s][:], in_=std_eps[s][:])
             for h in range(BANKS):

@@ -44,7 +44,8 @@ def tile_swintransformerblock_pb_s_kernel(
     nc = tc.nc
     with ExitStack() as ctx:
         keep = ctx.enter_context(tc.tile_pool(name="keep", bufs=1))
-        psum = ctx.enter_context(tc.psum_pool(name="psum", bufs=1))
+        psum_t = ctx.enter_context(tc.psum_pool(name="psum_t", bufs=1))
+        psum_mm = ctx.enter_context(tc.psum_pool(name="psum_mm", bufs=4))
         ctx.enter_context(tc.manual_schedule())
 
         def one_per_tile(pool, shape, dtype, name, align_bytes=None):
@@ -111,7 +112,7 @@ def tile_swintransformerblock_pb_s_kernel(
         )
         nc.vector.tensor_copy(out=by_image_row[:, :, 0:SHIFT], in_=by_window[:, 1, :, WIN - SHIFT : WIN])
 
-        bias_ps = psum.tile([P, CHANNELS], BF16)
+        bias_ps = psum_mm.tile([P, CHANNELS], BF16, tag="mm")
         for h in range(BANKS):
             cols = slice(BANK * h, BANK * (h + 1))
             nc.tensor.matmul(
@@ -120,30 +121,33 @@ def tile_swintransformerblock_pb_s_kernel(
         bias_all = keep.tile([P, CHANNELS], BF16)
         nc.vector.tensor_copy(out=bias_all[:], in_=bias_ps[:])
 
-        transposed = one_per_tile(psum, [P, PASSES, 2, P], F32, "transposed")
+        transposed = [one_per_tile(psum_t, [P, 2, P], F32, "transposed%d_" % g) for g in range(PASSES)]
         grouped = one_per_tile(keep, [P, PASSES * P * 4], BF16, "grouped", align_bytes=64)
         a_words = one_per_tile(keep, [P, PASSES * P], U32, "a_words", align_bytes=64)
         a_scales = one_per_tile(keep, [P, PASSES * P], U8, "a_scales", align_bytes=64)
         for s in tile_order:
             o_pairs = o_sb[s][:].bitcast(F32)
+            grouped_pairs = grouped[s][:].bitcast(F32).rearrange("p (g n u) -> p g n u", g=PASSES, u=2)
             for g in range(PASSES):
                 for u in range(2):
                     nc.tensor.transpose(
-                        transposed[s][:, g, u, :],
+                        transposed[g][s][:, u, :],
                         o_pairs[:, 2 * P * g + u : 2 * P * (g + 1) : 2],
                         perm[:],
                     )
-            nc.scalar.copy(
-                out=grouped[s][:].bitcast(F32).rearrange("p (g n u) -> p g n u", g=PASSES, u=2),
-                in_=transposed[s][:].rearrange("p g u n -> p g n u"),
-            )
+                nc.scalar.copy(
+                    out=grouped_pairs[:, g, :, :], in_=transposed[g][s][:].rearrange("p u n -> p n u")
+                )
         for s in tile_order:
-            nc.vector.quantize_mx(
-                out=a_words[s][:].bitcast(FP8X4), scales=a_scales[s][:], in_=grouped[s][:]
-            )
+            for g in range(PASSES):
+                nc.vector.quantize_mx(
+                    out=a_words[s][:, P * g : P * (g + 1)].bitcast(FP8X4),
+                    scales=a_scales[s][:, P * g : P * (g + 1)],
+                    in_=grouped[s][:, 4 * P * g : 4 * P * (g + 1)],
+                )
 
         acc = [
-            [psum.tile([P, BANK], F32, name="acc%d%d" % (s, h)) for h in range(BANKS)]
+            [psum_mm.tile([P, BANK], F32, name="acc%d%d" % (s, h), tag="mm") for h in range(BANKS)]
             for s in range(TILES)
         ]
         for s in tile_order:

@@ -44,8 +44,7 @@ def tile_swintransformerblock_pb_s_kernel(
     nc = tc.nc
     with ExitStack() as ctx:
         keep = ctx.enter_context(tc.tile_pool(name="keep", bufs=1))
-        psum_t = ctx.enter_context(tc.psum_pool(name="psum_t", bufs=1))
-        psum_mm = ctx.enter_context(tc.psum_pool(name="psum_mm", bufs=4))
+        psum = ctx.enter_context(tc.psum_pool(name="psum", bufs=1))
         ctx.enter_context(tc.manual_schedule())
 
         def one_per_tile(pool, shape, dtype, name, align_bytes=None):
@@ -82,17 +81,19 @@ def tile_swintransformerblock_pb_s_kernel(
         gain_bf = one_per_tile(keep, [P, 1], BF16, "gain_bf")
         offset_bf = one_per_tile(keep, [P, 1], BF16, "offset_bf")
         for s in tile_order:
+            for p0, t0, count in token_runs(s):
+                nc.sync.dma_start(out=x_sb[s][p0 : p0 + count, :], in_=x[0, t0 : t0 + count, :])
+            with nc.allow_non_contiguous_dma(reason="one 2-byte value for each partition"):
+                for p0, t0, count in token_runs(s):
+                    nc.sync.dma_start(
+                        out=offset_bf[s][p0 : p0 + count, :], in_=ada1_shift[0, t0 : t0 + count, :]
+                    )
+        for s in tile_order:
             with nc.allow_non_contiguous_dma(reason="one 2-byte value for each partition"):
                 for p0, t0, count in token_runs(s):
                     nc.sync.dma_start(
                         out=gain_bf[s][p0 : p0 + count, :], in_=ada1_scale[0, t0 : t0 + count, :]
                     )
-                for p0, t0, count in token_runs(s):
-                    nc.sync.dma_start(
-                        out=offset_bf[s][p0 : p0 + count, :], in_=ada1_shift[0, t0 : t0 + count, :]
-                    )
-            for p0, t0, count in token_runs(s):
-                nc.sync.dma_start(out=x_sb[s][p0 : p0 + count, :], in_=x[0, t0 : t0 + count, :])
 
         ones = keep.tile([P, P], BF16)
         nc.vector.memset(ones[:], 1.0)
@@ -112,42 +113,39 @@ def tile_swintransformerblock_pb_s_kernel(
         )
         nc.vector.tensor_copy(out=by_image_row[:, :, 0:SHIFT], in_=by_window[:, 1, :, WIN - SHIFT : WIN])
 
-        bias_ps = psum_mm.tile([P, CHANNELS], BF16, tag="mm")
-        for h in range(BANKS):
-            cols = slice(BANK * h, BANK * (h + 1))
-            nc.tensor.matmul(
-                out=bias_ps[:, cols], lhsT=ones[:], rhs=bias_rows[:, cols], start=True, stop=True
-            )
-        bias_all = keep.tile([P, CHANNELS], BF16)
-        nc.vector.tensor_copy(out=bias_all[:], in_=bias_ps[:])
-
-        transposed = [one_per_tile(psum_t, [P, 2, P], F32, "transposed%d_" % g) for g in range(PASSES)]
+        transposed = one_per_tile(psum, [P, PASSES, 2, P], F32, "transposed")
         grouped = one_per_tile(keep, [P, PASSES * P * 4], BF16, "grouped", align_bytes=64)
         a_words = one_per_tile(keep, [P, PASSES * P], U32, "a_words", align_bytes=64)
         a_scales = one_per_tile(keep, [P, PASSES * P], U8, "a_scales", align_bytes=64)
         for s in tile_order:
             o_pairs = o_sb[s][:].bitcast(F32)
-            grouped_pairs = grouped[s][:].bitcast(F32).rearrange("p (g n u) -> p g n u", g=PASSES, u=2)
             for g in range(PASSES):
                 for u in range(2):
                     nc.tensor.transpose(
-                        transposed[g][s][:, u, :],
+                        transposed[s][:, g, u, :],
                         o_pairs[:, 2 * P * g + u : 2 * P * (g + 1) : 2],
                         perm[:],
                     )
-                nc.scalar.copy(
-                    out=grouped_pairs[:, g, :, :], in_=transposed[g][s][:].rearrange("p u n -> p n u")
-                )
+            nc.scalar.copy(
+                out=grouped[s][:].bitcast(F32).rearrange("p (g n u) -> p g n u", g=PASSES, u=2),
+                in_=transposed[s][:].rearrange("p g u n -> p g n u"),
+            )
+        bias_ps = psum.tile([P, CHANNELS], BF16)
+        for h in range(BANKS):
+            cols = slice(BANK * h, BANK * (h + 1))
+            nc.tensor.matmul(
+                out=bias_ps[:, cols], lhsT=ones[:], rhs=bias_rows[:, cols], start=True, stop=True
+            )
+
         for s in tile_order:
-            for g in range(PASSES):
-                nc.vector.quantize_mx(
-                    out=a_words[s][:, P * g : P * (g + 1)].bitcast(FP8X4),
-                    scales=a_scales[s][:, P * g : P * (g + 1)],
-                    in_=grouped[s][:, 4 * P * g : 4 * P * (g + 1)],
-                )
+            nc.vector.quantize_mx(
+                out=a_words[s][:].bitcast(FP8X4), scales=a_scales[s][:], in_=grouped[s][:]
+            )
+        bias_all = keep.tile([P, CHANNELS], BF16)
+        nc.vector.tensor_copy(out=bias_all[:], in_=bias_ps[:])
 
         acc = [
-            [psum_mm.tile([P, BANK], F32, name="acc%d%d" % (s, h), tag="mm") for h in range(BANKS)]
+            [psum.tile([P, BANK], F32, name="acc%d%d" % (s, h)) for h in range(BANKS)]
             for s in range(TILES)
         ]
         for s in tile_order:
@@ -165,16 +163,21 @@ def tile_swintransformerblock_pb_s_kernel(
 
         x_offset = one_per_tile(keep, [P, CHANNELS], F32, "x_offset")
         gain = one_per_tile(keep, [P, 1], F32, "gain")
-        for s in tile_order:
-            nc.gpsimd.tensor_copy(out=gain[s][:], in_=gain_bf[s][:])
-            nc.gpsimd.tensor_scalar(
-                out=x_offset[s][:],
-                in0=x_sb[s][:],
-                scalar1=1.0,
-                scalar2=offset_bf[s][:],
-                op0=ALU.mult,
-                op1=ALU.add,
-            )
+        nc.scalar.activation(
+            out=x_offset[tile_order[0]][:],
+            in_=x_sb[tile_order[0]][:],
+            func=ACT.Identity,
+            bias=offset_bf[tile_order[0]][:],
+            scale=1.0,
+        )
+        nc.gpsimd.tensor_scalar(
+            out=x_offset[tile_order[1]][:],
+            in0=x_sb[tile_order[1]][:],
+            scalar1=1.0,
+            scalar2=offset_bf[tile_order[1]][:],
+            op0=ALU.mult,
+            op1=ALU.add,
+        )
 
         a_sb = one_per_tile(keep, [P, CHANNELS], F32, "a_sb")
         row_sums = one_per_tile(keep, [P, BANKS], F32, "row_sums")
@@ -214,6 +217,7 @@ def tile_swintransformerblock_pb_s_kernel(
             nc.scalar.activation(
                 out=std[s][:], in_=sum_squares[s][:], func=ACT.Sqrt, scale=1.0 / (CHANNELS - 1)
             )
+            nc.gpsimd.tensor_copy(out=gain[s][:], in_=gain_bf[s][:])
             nc.gpsimd.tensor_scalar(
                 out=centred[s][:],
                 in0=a_sb[s][:],

@@ -217,8 +217,8 @@ def tile_swintransformerblock_pb_s_kernel(
             nc.scalar.activation(
                 out=std[s][:], in_=sum_squares[s][:], func=ACT.Sqrt, scale=1.0 / (CHANNELS - 1)
             )
-            nc.gpsimd.tensor_copy(out=gain[s][:], in_=gain_bf[s][:])
-            nc.gpsimd.tensor_scalar(
+            nc.vector.tensor_copy(out=gain[s][:], in_=gain_bf[s][:])
+            nc.vector.tensor_scalar(
                 out=centred[s][:],
                 in0=a_sb[s][:],
                 scalar1=neg_mean[s][:],

@@ -217,8 +217,9 @@ def tile_swintransformerblock_pb_s_kernel(
             nc.scalar.activation(
                 out=std[s][:], in_=sum_squares[s][:], func=ACT.Sqrt, scale=1.0 / (CHANNELS - 1)
             )
-            nc.vector.tensor_copy(out=gain[s][:], in_=gain_bf[s][:])
-            nc.vector.tensor_scalar(
+            centring_engine = nc.gpsimd if s == tile_order[0] else nc.vector
+            centring_engine.tensor_copy(out=gain[s][:], in_=gain_bf[s][:])
+            centring_engine.tensor_scalar(
                 out=centred[s][:],
                 in0=a_sb[s][:],
                 scalar1=neg_mean[s][:],

@@ -27,6 +27,8 @@ PASSES = CHANNELS // K_PASS
 BANK = 512
 BANKS = CHANNELS // BANK
 
+WARM = 4
+
 FLOPS = 2 * TOKENS * CHANNELS * CHANNELS
 
 
@@ -55,6 +57,14 @@ def tile_swintransformerblock_pb_s_kernel(
 
         tile_order = [1, 0]
 
+        warm_src = keep.tile([P, P], F32)
+        nc.vector.memset(warm_src[:], 1.0)
+        warm_ps = psum.tile([P, WARM, P], F32, name="warm_ps", tag="acc%d%d" % (tile_order[1], 0))
+        for i in range(WARM):
+            nc.tensor.matmul(
+                out=warm_ps[:, i, :], lhsT=warm_src[:], rhs=warm_src[:], start=True, stop=True
+            )
+
         o_rows = o_attn.rearrange("w t c -> (w t) c")
         o_sb = one_per_tile(keep, [P, CHANNELS], BF16, "o_sb")
         for s in tile_order:
@@ -64,6 +74,19 @@ def tile_swintransformerblock_pb_s_kernel(
         nc.vector.memset(bias_rows[:].bitcast(I32), 0)
         nc.scalar.dma_start(out=bias_rows[0:1, :], in_=out_b.rearrange("(o c) -> o c", o=1))
 
+        w_words = [
+            keep.tile([P, PASSES, 2 * BANK], U8, name="w_words%d" % h, align_bytes=64)
+            for h in range(BANKS)
+        ]
+
+        def load_w_words(h):
+            nc.sync.dma_start(
+                out=w_words[h][:].bitcast(I32),
+                in_=out_w_words.rearrange("g p b -> p g b")[
+                    :, :, 2 * BANK * h : 2 * BANK * (h + 1)
+                ].bitcast(I32),
+            )
+
         w_scales = keep.tile([P, PASSES, CHANNELS], U8, align_bytes=64)
         nc.vector.memset(w_scales[:].bitcast(I32), 0)
         for r in range(4):
@@ -71,11 +94,8 @@ def tile_swintransformerblock_pb_s_kernel(
                 out=w_scales[r:P:32, :, :].bitcast(I32),
                 in_=out_w_scales[:, r:16:4, :].rearrange("g q n -> q g n").bitcast(I32),
             )
-        w_words = keep.tile([P, PASSES, 2 * CHANNELS], U8, align_bytes=64)
-        nc.sync.dma_start(
-            out=w_words[:].bitcast(I32),
-            in_=out_w_words.rearrange("g p b -> p g b").bitcast(I32),
-        )
+        load_w_words(0)
+        load_w_words(1)
 
         x_sb = one_per_tile(keep, [P, CHANNELS], BF16, "x_sb")
         gain_bf = one_per_tile(keep, [P, 1], BF16, "gain_bf")
@@ -113,53 +133,90 @@ def tile_swintransformerblock_pb_s_kernel(
         )
         nc.vector.tensor_copy(out=by_image_row[:, :, 0:SHIFT], in_=by_window[:, 1, :, WIN - SHIFT : WIN])
 
-        transposed = one_per_tile(psum, [P, PASSES, 2, P], F32, "transposed")
-        grouped = one_per_tile(keep, [P, PASSES * P * 4], BF16, "grouped", align_bytes=64)
-        a_words = one_per_tile(keep, [P, PASSES * P], U32, "a_words", align_bytes=64)
-        a_scales = one_per_tile(keep, [P, PASSES * P], U8, "a_scales", align_bytes=64)
-        for s in tile_order:
+        def per_pass(pool, shape, dtype, name, align_bytes=None):
+            return [
+                [
+                    pool.tile(shape, dtype, name="%s%d%d" % (name, s, g), align_bytes=align_bytes)
+                    for g in range(PASSES)
+                ]
+                for s in range(TILES)
+            ]
+
+        transposed = per_pass(psum, [P, 4, P], F32, "transposed")
+        grouped = per_pass(keep, [P, P * 4], BF16, "grouped", align_bytes=64)
+        a_words = per_pass(keep, [P, P], U32, "a_words", align_bytes=64)
+        a_scales = per_pass(keep, [P, P], U8, "a_scales", align_bytes=64)
+
+        def transpose_and_copy(s):
             o_pairs = o_sb[s][:].bitcast(F32)
             for g in range(PASSES):
                 for u in range(2):
                     nc.tensor.transpose(
-                        transposed[s][:, g, u, :],
+                        transposed[s][g][:, u, :],
                         o_pairs[:, 2 * P * g + u : 2 * P * (g + 1) : 2],
                         perm[:],
                     )
-            nc.scalar.copy(
-                out=grouped[s][:].bitcast(F32).rearrange("p (g n u) -> p g n u", g=PASSES, u=2),
-                in_=transposed[s][:].rearrange("p g u n -> p g n u"),
+            for g in range(PASSES):
+                nc.scalar.copy(
+                    out=grouped[s][g][:].bitcast(F32).rearrange("p (n u) -> p n u", u=2),
+                    in_=transposed[s][g][:, 0:2, :].rearrange("p u n -> p n u"),
+                )
+
+        def quantise(s, g):
+            nc.vector.quantize_mx(
+                out=a_words[s][g][:].bitcast(FP8X4), scales=a_scales[s][g][:], in_=grouped[s][g][:]
             )
-        bias_ps = psum.tile([P, CHANNELS], BF16)
+
+        acc = [[None for h in range(BANKS)] for s in range(TILES)]
+
+        def project(s, h):
+            acc[s][h] = psum.tile([P, BANK], F32, name="acc%d%d" % (s, h), tag="acc%d%d" % (s, h))
+            for g in range(PASSES):
+                nc.tensor.matmul_mx(
+                    out=acc[s][h][:],
+                    lhsT=a_words[s][g][:].bitcast(FP8X4),
+                    lhsT_scale=a_scales[s][g][:],
+                    rhs=w_words[h][:, g, :].bitcast(FP4X4),
+                    rhs_scale=w_scales[:, g, BANK * h : BANK * (h + 1)],
+                    start=(g == 0),
+                    stop=(g == PASSES - 1),
+                )
+
+        a_sb = one_per_tile(keep, [P, CHANNELS], F32, "a_sb")
+        row_sums = one_per_tile(keep, [P, BANKS], F32, "row_sums")
+
+        def add_bias(s, h):
+            cols = slice(BANK * h, BANK * (h + 1))
+            nc.vector.scalar_tensor_tensor(
+                out=a_sb[s][:, cols],
+                in0=acc[s][h][:],
+                scalar=1.0,
+                in1=bias_all[:, cols],
+                op0=ALU.mult,
+                op1=ALU.add,
+                accum_out=row_sums[s][:, h : h + 1],
+            )
+
+        first, last = tile_order
+        transpose_and_copy(first)
+        bias_ps = psum.tile([P, CHANNELS], BF16, name="bias_ps", tag="acc%d%d" % (last, BANKS - 1))
         for h in range(BANKS):
             cols = slice(BANK * h, BANK * (h + 1))
             nc.tensor.matmul(
                 out=bias_ps[:, cols], lhsT=ones[:], rhs=bias_rows[:, cols], start=True, stop=True
             )
-
-        for s in tile_order:
-            nc.vector.quantize_mx(
-                out=a_words[s][:].bitcast(FP8X4), scales=a_scales[s][:], in_=grouped[s][:]
-            )
+        transpose_and_copy(last)
+        quantise(first, 0)
+        quantise(first, 1)
         bias_all = keep.tile([P, CHANNELS], BF16)
         nc.vector.tensor_copy(out=bias_all[:], in_=bias_ps[:])
-
-        acc = [
-            [psum.tile([P, BANK], F32, name="acc%d%d" % (s, h)) for h in range(BANKS)]
-            for s in range(TILES)
-        ]
-        for s in tile_order:
-            for h in range(BANKS):
-                for g in range(PASSES):
-                    nc.tensor.matmul_mx(
-                        out=acc[s][h][:],
-                        lhsT=a_words[s][:, P * g : P * (g + 1)].bitcast(FP8X4),
-                        lhsT_scale=a_scales[s][:, P * g : P * (g + 1)],
-                        rhs=w_words[:, g, 2 * BANK * h : 2 * BANK * (h + 1)].bitcast(FP4X4),
-                        rhs_scale=w_scales[:, g, BANK * h : BANK * (h + 1)],
-                        start=(g == 0),
-                        stop=(g == PASSES - 1),
-                    )
+        quantise(last, 0)
+        project(first, 0)
+        add_bias(first, 0)
+        quantise(last, 1)
+        project(first, 1)
+        project(last, 0)
+        project(last, 1)
 
         x_offset = one_per_tile(keep, [P, CHANNELS], F32, "x_offset")
         gain = one_per_tile(keep, [P, 1], F32, "gain")
@@ -179,8 +236,6 @@ def tile_swintransformerblock_pb_s_kernel(
             op1=ALU.add,
         )
 
-        a_sb = one_per_tile(keep, [P, CHANNELS], F32, "a_sb")
-        row_sums = one_per_tile(keep, [P, BANKS], F32, "row_sums")
         neg_mean = one_per_tile(keep, [P, 1], F32, "neg_mean")
         squares = one_per_tile(keep, [P, CHANNELS], F32, "squares")
         sum_squares = one_per_tile(keep, [P, 1], F32, "sum_squares")
@@ -188,16 +243,8 @@ def tile_swintransformerblock_pb_s_kernel(
         std = one_per_tile(keep, [P, 1], F32, "std")
         for s in tile_order:
             for h in range(BANKS):
-                cols = slice(BANK * h, BANK * (h + 1))
-                nc.vector.scalar_tensor_tensor(
-                    out=a_sb[s][:, cols],
-                    in0=acc[s][h][:],
-                    scalar=1.0,
-                    in1=bias_all[:, cols],
-                    op0=ALU.mult,
-                    op1=ALU.add,
-                    accum_out=row_sums[s][:, h : h + 1],
-                )
+                if (s, h) != (first, 0):
+                    add_bias(s, h)
             nc.vector.tensor_scalar(
                 out=neg_mean[s][:],
                 in0=row_sums[s][:, 0:1],

@@ -65,14 +65,14 @@ def tile_swintransformerblock_pb_s_kernel(
                 out=warm_ps[:, i, :], lhsT=warm_src[:], rhs=warm_src[:], start=True, stop=True
             )
 
+        bias_rows = keep.tile([P, CHANNELS], BF16)
+        nc.vector.memset(bias_rows[:].bitcast(I32), 0)
+        nc.scalar.dma_start(out=bias_rows[0:1, :], in_=out_b.rearrange("(o c) -> o c", o=1))
+
         o_rows = o_attn.rearrange("w t c -> (w t) c")
         o_sb = one_per_tile(keep, [P, CHANNELS], BF16, "o_sb")
         for s in tile_order:
             nc.sync.dma_start(out=o_sb[s][:], in_=o_rows[P * s : P * (s + 1), :])
-
-        bias_rows = keep.tile([P, CHANNELS], BF16)
-        nc.vector.memset(bias_rows[:].bitcast(I32), 0)
-        nc.scalar.dma_start(out=bias_rows[0:1, :], in_=out_b.rearrange("(o c) -> o c", o=1))
 
         w_words = [
             keep.tile([P, PASSES, 2 * BANK], U8, name="w_words%d" % h, align_bytes=64)

from contextlib import ExitStack

import concourse.mybir as mybir
from concourse.masks import make_identity

F32 = mybir.dt.float32
BF16 = mybir.dt.bfloat16
I32 = mybir.dt.int32
U32 = mybir.dt.uint32
U8 = mybir.dt.uint8
FP8X4 = mybir.dt.float8_e4m3fn_x4
FP4X4 = mybir.dt.float4_e2m1fn_x4
ALU = mybir.AluOpType
ACT = mybir.ActivationFunctionType

P = 128
GRID = 16
WIN = 8
SHIFT = 4
TOKENS = GRID * GRID
CHANNELS = 1024
EPS = 1e-5

TILES = TOKENS // P
K_PASS = 4 * P
PASSES = CHANNELS // K_PASS
BANK = 512
BANKS = CHANNELS // BANK

WARM = 4

FLOPS = 2 * TOKENS * CHANNELS * CHANNELS


def token_runs(s):
    first = P * s + SHIFT * GRID
    if first + P <= TOKENS:
        return [(0, first, P)]
    head = TOKENS - first
    return [(0, first, head), (head, 0, P - head)]


def tile_swintransformerblock_pb_s_kernel(
    tc, o_attn, out_w_words, out_w_scales, out_b, ada1_scale, ada1_shift, x, out
):
    nc = tc.nc
    with ExitStack() as ctx:
        keep = ctx.enter_context(tc.tile_pool(name="keep", bufs=1))
        psum = ctx.enter_context(tc.psum_pool(name="psum", bufs=1))
        ctx.enter_context(tc.manual_schedule())

        def one_per_tile(pool, shape, dtype, name, align_bytes=None):
            return [
                pool.tile(shape, dtype, name="%s%d" % (name, s), align_bytes=align_bytes)
                for s in range(TILES)
            ]

        tile_order = [1, 0]

        warm_src = keep.tile([P, P], F32)
        nc.vector.memset(warm_src[:], 1.0)
        warm_ps = psum.tile([P, WARM, P], F32, name="warm_ps", tag="acc%d%d" % (tile_order[1], 0))
        for i in range(WARM):
            nc.tensor.matmul(
                out=warm_ps[:, i, :], lhsT=warm_src[:], rhs=warm_src[:], start=True, stop=True
            )

        bias_rows = keep.tile([P, CHANNELS], BF16)
        nc.vector.memset(bias_rows[:].bitcast(I32), 0)
        nc.scalar.dma_start(out=bias_rows[0:1, :], in_=out_b.rearrange("(o c) -> o c", o=1))

        o_rows = o_attn.rearrange("w t c -> (w t) c")
        o_sb = one_per_tile(keep, [P, CHANNELS], BF16, "o_sb")
        for s in tile_order:
            nc.sync.dma_start(out=o_sb[s][:], in_=o_rows[P * s : P * (s + 1), :])

        w_words = [
            keep.tile([P, PASSES, 2 * BANK], U8, name="w_words%d" % h, align_bytes=64)
            for h in range(BANKS)
        ]

        def load_w_words(h):
            nc.sync.dma_start(
                out=w_words[h][:].bitcast(I32),
                in_=out_w_words.rearrange("g p b -> p g b")[
                    :, :, 2 * BANK * h : 2 * BANK * (h + 1)
                ].bitcast(I32),
            )

        w_scales = keep.tile([P, PASSES, CHANNELS], U8, align_bytes=64)
        nc.vector.memset(w_scales[:].bitcast(I32), 0)
        for r in range(4):
            nc.sync.dma_start(
                out=w_scales[r:P:32, :, :].bitcast(I32),
                in_=out_w_scales[:, r:16:4, :].rearrange("g q n -> q g n").bitcast(I32),
            )
        load_w_words(0)
        load_w_words(1)

        x_sb = one_per_tile(keep, [P, CHANNELS], BF16, "x_sb")
        gain_bf = one_per_tile(keep, [P, 1], BF16, "gain_bf")
        offset_bf = one_per_tile(keep, [P, 1], BF16, "offset_bf")
        for s in tile_order:
            for p0, t0, count in token_runs(s):
                nc.sync.dma_start(out=x_sb[s][p0 : p0 + count, :], in_=x[0, t0 : t0 + count, :])
            with nc.allow_non_contiguous_dma(reason="one 2-byte value for each partition"):
                for p0, t0, count in token_runs(s):
                    nc.sync.dma_start(
                        out=offset_bf[s][p0 : p0 + count, :], in_=ada1_shift[0, t0 : t0 + count, :]
                    )
        for s in tile_order:
            with nc.allow_non_contiguous_dma(reason="one 2-byte value for each partition"):
                for p0, t0, count in token_runs(s):
                    nc.sync.dma_start(
                        out=gain_bf[s][p0 : p0 + count, :], in_=ada1_scale[0, t0 : t0 + count, :]
                    )

        ones = keep.tile([P, P], BF16)
        nc.vector.memset(ones[:], 1.0)
        one_col = keep.tile([P, 1], F32)
        nc.vector.memset(one_col[:], 1.0)
        sqrt_warm = keep.tile([P, 1], F32)
        nc.scalar.activation(out=sqrt_warm[:], in_=one_col[:], func=ACT.Sqrt)

        ident = keep.tile([P, P], F32)
        make_identity(nc, ident[:])
        perm = keep.tile([P, P], F32)
        by_window = ident[:].rearrange("p (wj r c) -> p wj r c", wj=2, r=WIN)
        by_image_row = perm[:].rearrange("p (r j) -> p r j", j=GRID)
        nc.vector.tensor_copy(out=by_image_row[:, :, SHIFT : SHIFT + WIN], in_=by_window[:, 0, :, :])
        nc.vector.tensor_copy(
            out=by_image_row[:, :, SHIFT + WIN : GRID], in_=by_window[:, 1, :, 0 : WIN - SHIFT]
        )
        nc.vector.tensor_copy(out=by_image_row[:, :, 0:SHIFT], in_=by_window[:, 1, :, WIN - SHIFT : WIN])

        def per_pass(pool, shape, dtype, name, align_bytes=None):
            return [
                [
                    pool.tile(shape, dtype, name="%s%d%d" % (name, s, g), align_bytes=align_bytes)
                    for g in range(PASSES)
                ]
                for s in range(TILES)
            ]

        transposed = per_pass(psum, [P, 4, P], F32, "transposed")
        grouped = per_pass(keep, [P, P * 4], BF16, "grouped", align_bytes=64)
        a_words = per_pass(keep, [P, P], U32, "a_words", align_bytes=64)
        a_scales = per_pass(keep, [P, P], U8, "a_scales", align_bytes=64)

        def transpose_and_copy(s):
            o_pairs = o_sb[s][:].bitcast(F32)
            for g in range(PASSES):
                for u in range(2):
                    nc.tensor.transpose(
                        transposed[s][g][:, u, :],
                        o_pairs[:, 2 * P * g + u : 2 * P * (g + 1) : 2],
                        perm[:],
                    )
            for g in range(PASSES):
                nc.scalar.copy(
                    out=grouped[s][g][:].bitcast(F32).rearrange("p (n u) -> p n u", u=2),
                    in_=transposed[s][g][:, 0:2, :].rearrange("p u n -> p n u"),
                )

        def quantise(s, g):
            nc.vector.quantize_mx(
                out=a_words[s][g][:].bitcast(FP8X4), scales=a_scales[s][g][:], in_=grouped[s][g][:]
            )

        acc = [[None for h in range(BANKS)] for s in range(TILES)]

        def project(s, h):
            acc[s][h] = psum.tile([P, BANK], F32, name="acc%d%d" % (s, h), tag="acc%d%d" % (s, h))
            for g in range(PASSES):
                nc.tensor.matmul_mx(
                    out=acc[s][h][:],
                    lhsT=a_words[s][g][:].bitcast(FP8X4),
                    lhsT_scale=a_scales[s][g][:],
                    rhs=w_words[h][:, g, :].bitcast(FP4X4),
                    rhs_scale=w_scales[:, g, BANK * h : BANK * (h + 1)],
                    start=(g == 0),
                    stop=(g == PASSES - 1),
                )

        a_sb = one_per_tile(keep, [P, CHANNELS], F32, "a_sb")
        row_sums = one_per_tile(keep, [P, BANKS], F32, "row_sums")

        def add_bias(s, h):
            cols = slice(BANK * h, BANK * (h + 1))
            nc.vector.scalar_tensor_tensor(
                out=a_sb[s][:, cols],
                in0=acc[s][h][:],
                scalar=1.0,
                in1=bias_all[:, cols],
                op0=ALU.mult,
                op1=ALU.add,
                accum_out=row_sums[s][:, h : h + 1],
            )

        first, last = tile_order
        transpose_and_copy(first)
        bias_ps = psum.tile([P, CHANNELS], BF16, name="bias_ps", tag="acc%d%d" % (last, BANKS - 1))
        for h in range(BANKS):
            cols = slice(BANK * h, BANK * (h + 1))
            nc.tensor.matmul(
                out=bias_ps[:, cols], lhsT=ones[:], rhs=bias_rows[:, cols], start=True, stop=True
            )
        transpose_and_copy(last)
        quantise(first, 0)
        quantise(first, 1)
        bias_all = keep.tile([P, CHANNELS], BF16)
        nc.vector.tensor_copy(out=bias_all[:], in_=bias_ps[:])
        quantise(last, 0)
        project(first, 0)
        add_bias(first, 0)
        quantise(last, 1)
        project(first, 1)
        project(last, 0)
        project(last, 1)

        x_offset = one_per_tile(keep, [P, CHANNELS], F32, "x_offset")
        gain = one_per_tile(keep, [P, 1], F32, "gain")
        nc.scalar.activation(
            out=x_offset[tile_order[0]][:],
            in_=x_sb[tile_order[0]][:],
            func=ACT.Identity,
            bias=offset_bf[tile_order[0]][:],
            scale=1.0,
        )
        nc.gpsimd.tensor_scalar(
            out=x_offset[tile_order[1]][:],
            in0=x_sb[tile_order[1]][:],
            scalar1=1.0,
            scalar2=offset_bf[tile_order[1]][:],
            op0=ALU.mult,
            op1=ALU.add,
        )

        neg_mean = one_per_tile(keep, [P, 1], F32, "neg_mean")
        squares = one_per_tile(keep, [P, CHANNELS], F32, "squares")
        sum_squares = one_per_tile(keep, [P, 1], F32, "sum_squares")
        centred = one_per_tile(keep, [P, CHANNELS], F32, "centred")
        std = one_per_tile(keep, [P, 1], F32, "std")
        for s in tile_order:
            for h in range(BANKS):
                if (s, h) != (first, 0):
                    add_bias(s, h)
            nc.vector.tensor_scalar(
                out=neg_mean[s][:],
                in0=row_sums[s][:, 0:1],
                scalar1=row_sums[s][:, 1:2],
                scalar2=-1.0 / CHANNELS,
                op0=ALU.add,
                op1=ALU.mult,
            )
            nc.scalar.activation(
                out=squares[s][:],
                in_=a_sb[s][:],
                func=ACT.Square,
                bias=neg_mean[s][:],
                scale=1.0,
                accum_out=sum_squares[s][:],
            )
            nc.scalar.activation(
                out=std[s][:], in_=sum_squares[s][:], func=ACT.Sqrt, scale=1.0 / (CHANNELS - 1)
            )
            centring_engine = nc.gpsimd if s == tile_order[0] else nc.vector
            centring_engine.tensor_copy(out=gain[s][:], in_=gain_bf[s][:])
            centring_engine.tensor_scalar(
                out=centred[s][:],
                in0=a_sb[s][:],
                scalar1=neg_mean[s][:],
                scalar2=gain[s][:],
                op0=ALU.add,
                op1=ALU.mult,
            )

        std_eps = one_per_tile(keep, [P, 1], F32, "std_eps")
        inv_std = one_per_tile(keep, [P, 1], F32, "inv_std")
        result = one_per_tile(keep, [P, CHANNELS], F32, "result")
        for s in tile_order:
            nc.vector.tensor_scalar_add(out=std_eps[s][:], in0=std[s][:], scalar1=EPS)
            nc.vector.reciprocal(out=inv_std[s][:], in_=std_eps[s][:])
            for h in range(BANKS):
                cols = slice(BANK * h, BANK * (h + 1))
                nc.vector.scalar_tensor_tensor(
                    out=result[s][:, cols],
                    in0=centred[s][:, cols],
                    scalar=inv_std[s][:],
                    in1=x_offset[s][:, cols],
                    op0=ALU.mult,
                    op1=ALU.add,
                )
                for p0, t0, count in token_runs(s):
                    nc.sync.dma_start(
                        out=out[0, t0 : t0 + count, cols], in_=result[s][p0 : p0 + count, cols]
                    )
